import numpy as np
import ml_dtypes


def mxq(x, axis, fmt="e4m3"):
    dtype, down = {"e4m3": (ml_dtypes.float8_e4m3fn, 7), "e5m2": (ml_dtypes.float8_e5m2, 14)}[fmt]
    v = np.moveaxis(np.asarray(x, np.float32).astype(ml_dtypes.bfloat16).astype(np.float64), axis, -1)
    blocks = v.reshape(v.shape[:-1] + (-1, 32))
    amax = np.abs(blocks).max(-1, keepdims=True)
    byte = np.maximum(np.where(amax > 0, np.frexp(amax)[1] - 1 + 127, 0) - down, 1)
    scale = np.exp2(byte - 127.0)
    codes = (blocks / scale).astype(np.float32).astype(dtype).astype(np.float64)
    return np.moveaxis((codes * scale).reshape(v.shape), -1, axis)


WIDE = False


def mx_kscale(k):
    if not WIDE:
        return np.ones(k)
    levels = np.array([10, -10, 5, -5, 0])
    a = np.random.permutation(np.resize(levels, k // 512 * 4)).reshape(k // 512, 4)
    idx = np.arange(k)
    return np.exp2(a[idx // 512, idx % 128 // 32])


BF16 = ml_dtypes.bfloat16


def bf(x):
    return np.asarray(x, np.float32).astype(BF16)


def f64(x):
    return np.asarray(x).astype(np.float64)


B, S, D, V = 2, 128, 1024, 8192
LN_EPS = 1e-5


def layer_norm(x, gamma, beta):
    mu = np.mean(x, axis=-1, keepdims=True)
    var = np.mean(np.square(x - mu), axis=-1, keepdims=True)
    return (x - mu) * (1.0 / np.sqrt(var + LN_EPS)) * gamma + beta


def setup_inputs():
    t = mx_kscale(V)
    return {"enc_out": bf(np.random.standard_normal((B, S, D))),
            "proj_w": bf(np.random.standard_normal((V, D)) * 0.075),
            "proj_b": bf(np.random.standard_normal(V) * 0.5 + np.log(t)),
            "emb": bf(np.random.standard_normal((V, D)) * 2.0 * np.mean(t) / t[:, None]),
            "ln_gamma": bf(1.0 + 0.1 * np.random.standard_normal(D)),
            "ln_beta": bf(0.1 * np.random.standard_normal(D))}


def reference(enc_out, proj_w, proj_b, emb, ln_gamma, ln_beta):
    x = f64(enc_out)
    logits = (mxq(x, 2, "e4m3") @ mxq(f64(proj_w), 1, "e4m3").T) + f64(proj_b)
    e = np.exp(logits - logits.max(-1, keepdims=True))
    soft_emb = (mxq(e, 2, "e4m3") @ mxq(f64(emb), 0, "e4m3")) / e.sum(-1, keepdims=True)
    return layer_norm(x + soft_emb, f64(ln_gamma), f64(ln_beta))

@@ -1,0 +1,308 @@
+from contextlib import ExitStack
+
+import concourse.mybir as mybir
+from concourse.masks import make_identity
+
+F32 = mybir.dt.float32
+BF16 = mybir.dt.bfloat16
+U32 = mybir.dt.uint32
+U8 = mybir.dt.uint8
+FP8X4 = mybir.dt.float8_e4m3fn_x4
+ALU = mybir.AluOpType
+ACT = mybir.ActivationFunctionType
+AX = mybir.AxisListType
+
+P = 128
+T_TILES = 2
+D = 1024
+V = 8192
+CHUNK = 512
+N_CHUNKS = V // CHUNK
+N_PASSES = V // 512
+UNIT = 1024
+N_UNITS = V // UNIT
+LN_EPS = 1e-5
+
+FLOPS = 2 * 2 * 256 * V * D
+
+LATE_ENGINE = ["v", "v", "v", "v", "v", "s", "v", "v", "v", "v", "v", "v"]
+
+
+def tile_probabilisticencoder_kernel(tc, enc_out, proj_w, proj_b, emb, ln_gamma, ln_beta, out):
+    nc = tc.nc
+    x_dram = enc_out.flatten_outer_dims()
+    out_dram = out.flatten_outer_dims()
+
+    with ExitStack() as ctx:
+        const = ctx.enter_context(tc.tile_pool(name="const", bufs=1))
+        work = ctx.enter_context(tc.tile_pool(name="work", bufs=2))
+        psum = ctx.enter_context(tc.psum_pool(name="psum", bufs=4))
+
+        x_sb = const.tile([P, T_TILES, D], BF16, name="x_sb")
+        nc.sync.dma_start(out=x_sb[:], in_=x_dram.rearrange("(a p) d -> p a d", p=P))
+
+        ident_f = const.tile([P, P], F32, name="ident_f")
+        make_identity(nc, ident_f[:])
+        ident_b = const.tile([P, P], BF16, name="ident_b")
+        make_identity(nc, ident_b[:])
+
+        small = const.tile([P, 4], F32, name="small")
+        nc.vector.memset(small[:, 0:1], 0.0)
+        nc.vector.memset(small[:, 1:2], LN_EPS)
+        junk = const.tile([P, 2], F32, name="junk")
+        nc.scalar.activation(out=junk[:, 0:1], in_=small[:, 0:1], func=ACT.Exp)
+
+        logits = const.tile([P, T_TILES, V], F32, name="logits")
+        chunk_max = const.tile([P, T_TILES, N_CHUNKS], F32, name="chunk_max")
+        part_sum = const.tile([P, T_TILES, N_UNITS], F32, name="part_sum")
+        e_codes = const.tile([P, N_UNITS * 512], U32, name="e_codes", align_bytes=64)
+        e_scales = const.tile([P, N_UNITS * 512], U8, name="e_scales", align_bytes=64)
+        x_codes = const.tile([P, 512], U32, name="x_codes", align_bytes=64)
+        x_scales = const.tile([P, 512], U8, name="x_scales", align_bytes=64)
+        gamma_bc = const.tile([P, D], BF16, name="gamma_bc")
+        beta_bc = const.tile([P, D], BF16, name="beta_bc")
+
+        w_raw = {}
+        m_raw = {}
+        bias_bc = {}
+
+        def load_w(c):
+            t = work.tile([P, 4, D], BF16, name="w_raw%d" % c, tag="raw", bufs=5)
+            nc.sync.dma_start(
+                out=t[:], in_=proj_w[c * CHUNK:(c + 1) * CHUNK, :].rearrange("(i q) k -> q i k", q=P)
+            )
+            w_raw[c] = t
+
+        def load_m(g):
+            t = work.tile([P, 4, D], BF16, name="m_raw%d" % g, tag="raw", bufs=5)
+            nc.sync.dma_start(
+                out=t[:], in_=emb[g * 512:(g + 1) * 512, :].rearrange("(j p) d -> p j d", p=P)
+            )
+            m_raw[g] = t
+
+        def load_bias(s):
+            t = work.tile([P, 2048], BF16, name="bias%d" % s, tag="bias", bufs=2)
+            nc.gpsimd.dma_start(out=t[:], in_=proj_b[s * 2048:(s + 1) * 2048].partition_broadcast(P))
+            bias_bc[s] = t
+
+        load_w(0)
+        load_bias(0)
+        load_w(1)
+        load_w(2)
+        load_m(0)
+        load_bias(1)
+
+        x_grp = work.tile([P, 2, T_TILES, P, 4], BF16, name="x_grp", tag="egrp", bufs=2, align_bytes=64)
+        x_grp32 = x_grp[:].bitcast(F32)
+        for a in range(T_TILES):
+            xt = psum.tile([P, 4, P], F32, name="xt%d" % a, tag="tp")
+            xw = x_sb[:, a, :].bitcast(F32)
+            for u in range(4):
+                nc.tensor.transpose(xt[:, u, :], xw[:, u * P:(u + 1) * P], ident_f[:])
+            nc.scalar.copy(out=x_grp32[:, :, a, :, :], in_=xt[:].rearrange("p (g u) t -> p g t u", g=2))
+        nc.vector.quantize_mx(
+            out=x_codes[:].bitcast(FP8X4),
+            scales=x_scales[:],
+            in_=x_grp[:].rearrange("p g a t j -> p (g a t j)"),
+        )
+
+        w_banks = {}
+        w_grp = {}
+        w_codes = {}
+        w_scales = {}
+
+        def w_transpose(c):
+            banks = []
+            for i in range(4):
+                tp = psum.tile([P, 4, P], F32, name="wt%d_%d" % (c, i), tag="tp")
+                ww = w_raw[c][:, i, :].bitcast(F32)
+                for u in range(4):
+                    nc.tensor.transpose(tp[:, u, :], ww[:, u * P:(u + 1) * P], ident_f[:])
+                banks.append(tp)
+            w_banks[c] = banks
+
+        def w_copy_out(c):
+            g = work.tile([P, 2, CHUNK, 4], BF16, name="w_grp%d" % c, tag="grp", bufs=3, align_bytes=64)
+            g32 = g[:].bitcast(F32)
+            for i in range(4):
+                nc.scalar.copy(
+                    out=g32[:, :, i * P:(i + 1) * P, :],
+                    in_=w_banks[c][i][:].rearrange("p (g u) q -> p g q u", g=2),
+                )
+            w_grp[c] = g
+
+        def w_quantise(c):
+            q = work.tile([P, 2 * CHUNK], U32, name="w_codes%d" % c, tag="wq", bufs=2, align_bytes=64)
+            s = work.tile([P, 2 * CHUNK], U8, name="w_scales%d" % c, tag="ws", bufs=2, align_bytes=64)
+            nc.vector.quantize_mx(
+                out=q[:].bitcast(FP8X4), scales=s[:], in_=w_grp[c][:].rearrange("p g v j -> p (g v j)")
+            )
+            w_codes[c] = q
+            w_scales[c] = s
+
+        def stage1(c):
+            bias_t = bias_bc[c // 4]
+            off = (c % 4) * CHUNK
+            for a in range(T_TILES):
+                lg = psum.tile([P, CHUNK], F32, name="lg%d_%d" % (c, a), tag="mm")
+                for g in range(2):
+                    lo = (g * T_TILES + a) * P
+                    nc.tensor.matmul_mx(
+                        out=lg[:],
+                        lhsT=x_codes[:, lo:lo + P].bitcast(FP8X4),
+                        lhsT_scale=x_scales[:, lo:lo + P],
+                        rhs=w_codes[c][:, g * CHUNK:(g + 1) * CHUNK].bitcast(FP8X4),
+                        rhs_scale=w_scales[c][:, g * CHUNK:(g + 1) * CHUNK],
+                        start=(g == 0),
+                        stop=(g == 1),
+                    )
+                nc.vector.tensor_tensor(
+                    out=logits[:, a, c * CHUNK:(c + 1) * CHUNK],
+                    in0=lg[:],
+                    in1=bias_t[:, off:off + CHUNK],
+                    op=ALU.add,
+                )
+            nc.vector.tensor_reduce(
+                out=chunk_max[:, :, c], in_=logits[:, :, c * CHUNK:(c + 1) * CHUNK], axis=AX.X, op=ALU.max
+            )
+
+        m_grp = {}
+        m_codes = {}
+        m_scales = {}
+
+        def m_regroup(g, engine, d0, d1):
+            if g not in m_grp:
+                m_grp[g] = work.tile([P, D, 4], BF16, name="m_grp%d" % g, tag="grp", bufs=3, align_bytes=64)
+            dst = m_grp[g][:, d0:d1, :].rearrange("p (c i) t -> p c t i", i=4)
+            src = m_raw[g][:, :, d0:d1].rearrange("p t (c i) -> p c t i", i=4)
+            if engine == "s":
+                nc.scalar.copy(out=dst, in_=src)
+            else:
+                nc.vector.tensor_copy(out=dst, in_=src)
+
+        def m_quantise(g):
+            q = work.tile([P, D], U32, name="m_codes%d" % g, tag="mq", bufs=6, align_bytes=64)
+            s = work.tile([P, D], U8, name="m_scales%d" % g, tag="ms", bufs=6, align_bytes=64)
+            nc.vector.quantize_mx(
+                out=q[:].bitcast(FP8X4), scales=s[:], in_=m_grp[g][:].rearrange("p d j -> p (d j)")
+            )
+            m_codes[g] = q
+            m_scales[g] = s
+
+        w_transpose(0)
+        w_copy_out(0)
+        w_quantise(0)
+        for c in range(N_CHUNKS):
+            if c + 3 < N_CHUNKS:
+                load_w(c + 3)
+            if c % 4 == 1 and c // 4 + 1 < 5:
+                load_m(c // 4 + 1)
+            if c % 4 == 0 and 2 <= c // 4 + 1 < 4:
+                load_bias(c // 4 + 1)
+            if c + 1 < N_CHUNKS:
+                w_transpose(c + 1)
+                w_copy_out(c + 1)
+            m_regroup(c // 4, "s", (c % 4) * 256, (c % 4 + 1) * 256)
+            if c + 1 < N_CHUNKS:
+                w_quantise(c + 1)
+            stage1(c)
+            if c % 4 == 3:
+                m_quantise(c // 4)
+
+        nc.gpsimd.dma_start(out=gamma_bc[:], in_=ln_gamma.partition_broadcast(P))
+        nc.gpsimd.dma_start(out=beta_bc[:], in_=ln_beta.partition_broadcast(P))
+
+        row_max = const.tile([P, T_TILES], F32, name="row_max")
+        neg_max = const.tile([P, T_TILES], F32, name="neg_max")
+        nc.vector.tensor_reduce(out=row_max[:], in_=chunk_max[:], axis=AX.X, op=ALU.max)
+        nc.vector.tensor_scalar(out=neg_max[:], in0=row_max[:], scalar1=-1.0, scalar2=None, op0=ALU.mult)
+
+        acc = {}
+        for a in range(T_TILES):
+            for h in range(2):
+                acc[(a, h)] = psum.tile([P, 512], F32, name="acc%d_%d" % (a, h), tag="mm")
+
+        def stage2(g):
+            for a in range(T_TILES):
+                lo = (g * T_TILES + a) * P
+                for h in range(2):
+                    nc.tensor.matmul_mx(
+                        out=acc[(a, h)][:],
+                        lhsT=e_codes[:, lo:lo + P].bitcast(FP8X4),
+                        lhsT_scale=e_scales[:, lo:lo + P],
+                        rhs=m_codes[g][:, h * 512:(h + 1) * 512].bitcast(FP8X4),
+                        rhs_scale=m_scales[g][:, h * 512:(h + 1) * 512],
+                        start=(g == 0),
+                        stop=(g == N_PASSES - 1),
+                    )
+
+        def late_pass(g):
+            if g + 1 < N_PASSES:
+                load_m(g + 1)
+            m_regroup(g, LATE_ENGINE[g - 4], 0, D)
+            m_quantise(g)
+
+        for n in range(N_UNITS):
+            e_sb = work.tile([P, T_TILES, UNIT], BF16, name="e_sb%d" % n, tag="e_sb", bufs=3)
+            for a in range(T_TILES):
+                nc.scalar.activation(
+                    out=e_sb[:, a, :],
+                    in_=logits[:, a, n * UNIT:(n + 1) * UNIT],
+                    func=ACT.Exp,
+                    bias=neg_max[:, a:a + 1],
+                    scale=1.0,
+                    accum_out=part_sum[:, a, n:n + 1],
+                )
+            e_grp = work.tile([P, 2, T_TILES, P, 4], BF16, name="e_grp%d" % n, tag="egrp", bufs=2, align_bytes=64)
+            for k in range(2):
+                et = psum.tile([P, T_TILES, 4, P], BF16, name="et%d_%d" % (n, k), tag="tp")
+                for a in range(T_TILES):
+                    for j in range(4):
+                        lo = k * 512 + j * P
+                        nc.tensor.transpose(et[:, a, j, :], e_sb[:, a, lo:lo + P], ident_b[:])
+                nc.scalar.copy(out=e_grp[:, k, :, :, :], in_=et[:].rearrange("p a j t -> p a t j"))
+            nc.vector.quantize_mx(
+                out=e_codes[:, n * 512:(n + 1) * 512].bitcast(FP8X4),
+                scales=e_scales[:, n * 512:(n + 1) * 512],
+                in_=e_grp[:].rearrange("p k a t j -> p (k a t j)"),
+            )
+            if n < 6:
+                late_pass(4 + 2 * n)
+                late_pass(5 + 2 * n)
+            stage2(2 * n)
+            stage2(2 * n + 1)
+
+        nc.scalar.activation(out=junk[:, 1:2], in_=part_sum[:, 1, N_UNITS - 1:N_UNITS], func=ACT.Sqrt)
+
+        row_sum = const.tile([P, T_TILES], F32, name="row_sum")
+        row_inv = const.tile([P, T_TILES], F32, name="row_inv")
+        nc.vector.tensor_reduce(out=row_sum[:], in_=part_sum[:], axis=AX.X, op=ALU.add)
+        nc.vector.reciprocal(out=row_inv[:], in_=row_sum[:])
+
+        for a in range(T_TILES):
+            y = work.tile([P, D], F32, name="y%d" % a, tag="grp", bufs=3, align_bytes=64)
+            stats = const.tile([P, 2, 6], F32, name="stats%d" % a)
+            mv = const.tile([P, 2], F32, name="mv%d" % a)
+            std = const.tile([P, 1], F32, name="std%d" % a)
+            rstd = const.tile([P, 1], F32, name="rstd%d" % a)
+            for h in range(2):
+                nc.vector.scalar_tensor_tensor(
+                    out=y[:, h * 512:(h + 1) * 512],
+                    in0=acc[(a, h)][:],
+                    scalar=row_inv[:, a:a + 1],
+                    in1=x_sb[:, a, h * 512:(h + 1) * 512],
+                    op0=ALU.mult,
+                    op1=ALU.add,
+                )
+                nc.vector.bn_stats(out=stats[:, h, :], in_=y[:, h * 512:(h + 1) * 512])
+            nc.vector.bn_aggr(out=mv[:], in_=stats[:].rearrange("p h s -> p (h s)"))
+            nc.scalar.activation(out=std[:], in_=mv[:, 1:2], func=ACT.Sqrt, bias=small[:, 1:2], scale=1.0)
+            nc.vector.reciprocal(out=rstd[:], in_=std[:])
+            o = work.tile([P, D], F32, name="o%d" % a, tag="grp", bufs=3, align_bytes=64)
+            nc.vector.scalar_tensor_tensor(
+                out=o[:], in0=y[:], scalar=mv[:, 0:1], in1=gamma_bc[:], op0=ALU.subtract, op1=ALU.mult
+            )
+            nc.vector.scalar_tensor_tensor(
+                out=o[:], in0=o[:], scalar=rstd[:, 0:1], in1=beta_bc[:], op0=ALU.mult, op1=ALU.add
+            )
+            nc.sync.dma_start(out=out_dram[a * P:(a + 1) * P, :], in_=o[:])

@@ -25,7 +25,12 @@ LN_EPS = 1e-5
 
 FLOPS = 2 * 2 * 256 * V * D
 
-LATE_ENGINE = ["v", "v", "v", "v", "v", "s", "v", "v", "v", "v", "v", "v"]
+PINNED = True
+EARLY_PASSES = 4
+FIRST_BIAS_BANKS = 3
+PRE_STEPS = 3
+STEPS_PER_UNIT = [1, 1, 1, 2, 1, 1, 1, 1]
+LAST_ON_SCALAR = 1
 
 
 def tile_probabilisticencoder_kernel(tc, enc_out, proj_w, proj_b, emb, ln_gamma, ln_beta, out):
@@ -37,16 +42,29 @@ def tile_probabilisticencoder_kernel(tc, enc_out, proj_w, proj_b, emb, ln_gamma,
         const = ctx.enter_context(tc.tile_pool(name="const", bufs=1))
         work = ctx.enter_context(tc.tile_pool(name="work", bufs=2))
         psum = ctx.enter_context(tc.psum_pool(name="psum", bufs=4))
+        if PINNED:
+            ctx.enter_context(tc.manual_schedule())
+
+        def raw_tile(shape, name):
+            return work.tile(shape, BF16, name=name, tag="raw", bufs=6, align_bytes=64)
+
+        def grp_tile(shape, dtype, name):
+            return work.tile(shape, dtype, name=name, tag="grp", bufs=4, align_bytes=64)
 
         x_sb = const.tile([P, T_TILES, D], BF16, name="x_sb")
         nc.sync.dma_start(out=x_sb[:], in_=x_dram.rearrange("(a p) d -> p a d", p=P))
 
+        rows = const.tile([P, CHUNK], BF16, name="rows")
+        nc.vector.memset(rows[:], 0.0)
+        nc.scalar.dma_start(out=rows[0:16, :], in_=proj_b.rearrange("(c n) -> c n", n=CHUNK))
+        nc.scalar.dma_start(out=rows[16:18, :], in_=ln_gamma.rearrange("(c n) -> c n", n=CHUNK))
+        nc.scalar.dma_start(out=rows[18:20, :], in_=ln_beta.rearrange("(c n) -> c n", n=CHUNK))
         ident_f = const.tile([P, P], F32, name="ident_f")
         make_identity(nc, ident_f[:])
         ident_b = const.tile([P, P], BF16, name="ident_b")
         make_identity(nc, ident_b[:])
 
-        small = const.tile([P, 4], F32, name="small")
+        small = const.tile([P, 2], F32, name="small")
         nc.vector.memset(small[:, 0:1], 0.0)
         nc.vector.memset(small[:, 1:2], LN_EPS)
         junk = const.tile([P, 2], F32, name="junk")
@@ -55,44 +73,38 @@ def tile_probabilisticencoder_kernel(tc, enc_out, proj_w, proj_b, emb, ln_gamma,
         logits = const.tile([P, T_TILES, V], F32, name="logits")
         chunk_max = const.tile([P, T_TILES, N_CHUNKS], F32, name="chunk_max")
         part_sum = const.tile([P, T_TILES, N_UNITS], F32, name="part_sum")
-        e_codes = const.tile([P, N_UNITS * 512], U32, name="e_codes", align_bytes=64)
         e_scales = const.tile([P, N_UNITS * 512], U8, name="e_scales", align_bytes=64)
         x_codes = const.tile([P, 512], U32, name="x_codes", align_bytes=64)
         x_scales = const.tile([P, 512], U8, name="x_scales", align_bytes=64)
-        gamma_bc = const.tile([P, D], BF16, name="gamma_bc")
-        beta_bc = const.tile([P, D], BF16, name="beta_bc")
+        gb_bc = const.tile([P, 2, D], BF16, name="gb_bc")
+        bias_bc = work.tile([P, V], BF16, name="bias_bc", tag="b16", bufs=1, align_bytes=64)
 
         w_raw = {}
         m_raw = {}
-        bias_bc = {}
+        state = {"next_m": 0, "bias": 0, "pass": 0, "piece": 0, "quantised": 0}
 
         def load_w(c):
-            t = work.tile([P, 4, D], BF16, name="w_raw%d" % c, tag="raw", bufs=5)
+            t = raw_tile([P, 4, D], "w_raw%d" % c)
             nc.sync.dma_start(
-                out=t[:], in_=proj_w[c * CHUNK:(c + 1) * CHUNK, :].rearrange("(i q) k -> q i k", q=P)
+                out=t[:], in_=proj_w[c * CHUNK:(c + 1) * CHUNK, :].rearrange("(q i) k -> q i k", i=4)
             )
             w_raw[c] = t
 
-        def load_m(g):
-            t = work.tile([P, 4, D], BF16, name="m_raw%d" % g, tag="raw", bufs=5)
-            nc.sync.dma_start(
-                out=t[:], in_=emb[g * 512:(g + 1) * 512, :].rearrange("(j p) d -> p j d", p=P)
-            )
-            m_raw[g] = t
-
-        def load_bias(s):
-            t = work.tile([P, 2048], BF16, name="bias%d" % s, tag="bias", bufs=2)
-            nc.gpsimd.dma_start(out=t[:], in_=proj_b[s * 2048:(s + 1) * 2048].partition_broadcast(P))
-            bias_bc[s] = t
+        def load_m():
+            g = state["next_m"]
+            if g < N_PASSES:
+                t = raw_tile([P, 4, D], "m_raw%d" % g)
+                nc.sync.dma_start(
+                    out=t[:], in_=emb[g * 512:(g + 1) * 512, :].rearrange("(p j) d -> p j d", j=4)
+                )
+                m_raw[g] = t
+                state["next_m"] = g + 1
 
         load_w(0)
-        load_bias(0)
         load_w(1)
         load_w(2)
-        load_m(0)
-        load_bias(1)
 
-        x_grp = work.tile([P, 2, T_TILES, P, 4], BF16, name="x_grp", tag="egrp", bufs=2, align_bytes=64)
+        x_grp = grp_tile([P, 2, T_TILES, P, 4], BF16, "x_grp")
         x_grp32 = x_grp[:].bitcast(F32)
         for a in range(T_TILES):
             xt = psum.tile([P, 4, P], F32, name="xt%d" % a, tag="tp")
@@ -106,12 +118,36 @@ def tile_probabilisticencoder_kernel(tc, enc_out, proj_w, proj_b, emb, ln_gamma,
             in_=x_grp[:].rearrange("p g a t j -> p (g a t j)"),
         )
 
-        w_banks = {}
+        def spread_bank():
+            r = state["bias"]
+            if r >= 10:
+                return False
+            bank = psum.tile([P, 2 * CHUNK], BF16, name="bank%d" % r, tag="mm")
+            for h in range(2):
+                row = 2 * r + h
+                nc.tensor.matmul(
+                    out=bank[:, h * CHUNK:(h + 1) * CHUNK],
+                    lhsT=ident_b[:, row:row + 1].to_broadcast([P, P]),
+                    rhs=rows[:],
+                    start=True,
+                    stop=True,
+                )
+            if r < 8:
+                nc.scalar.copy(out=bias_bc[:, r * 1024:(r + 1) * 1024], in_=bank[:])
+            else:
+                nc.scalar.copy(out=gb_bc[:, r - 8, :], in_=bank[:])
+            state["bias"] = r + 1
+            return True
+
+        for r in range(FIRST_BIAS_BANKS):
+            spread_bank()
+
         w_grp = {}
         w_codes = {}
         w_scales = {}
+        lg = {}
 
-        def w_transpose(c):
+        def w_transpose_and_copy(c):
             banks = []
             for i in range(4):
                 tp = psum.tile([P, 4, P], F32, name="wt%d_%d" % (c, i), tag="tp")
@@ -119,108 +155,162 @@ def tile_probabilisticencoder_kernel(tc, enc_out, proj_w, proj_b, emb, ln_gamma,
                 for u in range(4):
                     nc.tensor.transpose(tp[:, u, :], ww[:, u * P:(u + 1) * P], ident_f[:])
                 banks.append(tp)
-            w_banks[c] = banks
-
-        def w_copy_out(c):
-            g = work.tile([P, 2, CHUNK, 4], BF16, name="w_grp%d" % c, tag="grp", bufs=3, align_bytes=64)
+            if c + 3 < N_CHUNKS:
+                load_w(c + 3)
+            g = grp_tile([P, 2, CHUNK, 4], BF16, "w_grp%d" % c)
             g32 = g[:].bitcast(F32)
             for i in range(4):
                 nc.scalar.copy(
                     out=g32[:, :, i * P:(i + 1) * P, :],
-                    in_=w_banks[c][i][:].rearrange("p (g u) q -> p g q u", g=2),
+                    in_=banks[i][:].rearrange("p (g u) q -> p g q u", g=2),
                 )
             w_grp[c] = g
 
-        def w_quantise(c):
+        def w_quantise_and_multiply(c):
             q = work.tile([P, 2 * CHUNK], U32, name="w_codes%d" % c, tag="wq", bufs=2, align_bytes=64)
             s = work.tile([P, 2 * CHUNK], U8, name="w_scales%d" % c, tag="ws", bufs=2, align_bytes=64)
             nc.vector.quantize_mx(
                 out=q[:].bitcast(FP8X4), scales=s[:], in_=w_grp[c][:].rearrange("p g v j -> p (g v j)")
             )
-            w_codes[c] = q
-            w_scales[c] = s
-
-        def stage1(c):
-            bias_t = bias_bc[c // 4]
-            off = (c % 4) * CHUNK
             for a in range(T_TILES):
-                lg = psum.tile([P, CHUNK], F32, name="lg%d_%d" % (c, a), tag="mm")
+                t = psum.tile([P, CHUNK], F32, name="lg%d_%d" % (c, a), tag="mm")
                 for g in range(2):
                     lo = (g * T_TILES + a) * P
                     nc.tensor.matmul_mx(
-                        out=lg[:],
+                        out=t[:],
                         lhsT=x_codes[:, lo:lo + P].bitcast(FP8X4),
                         lhsT_scale=x_scales[:, lo:lo + P],
-                        rhs=w_codes[c][:, g * CHUNK:(g + 1) * CHUNK].bitcast(FP8X4),
-                        rhs_scale=w_scales[c][:, g * CHUNK:(g + 1) * CHUNK],
+                        rhs=q[:, g * CHUNK:(g + 1) * CHUNK].bitcast(FP8X4),
+                        rhs_scale=s[:, g * CHUNK:(g + 1) * CHUNK],
                         start=(g == 0),
                         stop=(g == 1),
                     )
+                lg[(c, a)] = t
+
+        def add_bias_and_max(c):
+            cols = slice(c * CHUNK, (c + 1) * CHUNK)
+            for a in range(T_TILES):
                 nc.vector.tensor_tensor(
-                    out=logits[:, a, c * CHUNK:(c + 1) * CHUNK],
-                    in0=lg[:],
-                    in1=bias_t[:, off:off + CHUNK],
+                    out=logits[:, a, cols].rearrange("p (i q) -> p i q", i=4),
+                    in0=lg[(c, a)][:].rearrange("p (i q) -> p i q", i=4),
+                    in1=bias_bc[:, cols].rearrange("p (q i) -> p i q", i=4),
                     op=ALU.add,
                 )
-            nc.vector.tensor_reduce(
-                out=chunk_max[:, :, c], in_=logits[:, :, c * CHUNK:(c + 1) * CHUNK], axis=AX.X, op=ALU.max
-            )
+            nc.vector.tensor_reduce(out=chunk_max[:, :, c], in_=logits[:, :, cols], axis=AX.X, op=ALU.max)
 
         m_grp = {}
         m_codes = {}
         m_scales = {}
 
-        def m_regroup(g, engine, d0, d1):
+        def m_regroup(g, engine, d0, d1, last):
             if g not in m_grp:
-                m_grp[g] = work.tile([P, D, 4], BF16, name="m_grp%d" % g, tag="grp", bufs=3, align_bytes=64)
+                m_grp[g] = grp_tile([P, D, 4], BF16, "m_grp%d" % g)
             dst = m_grp[g][:, d0:d1, :].rearrange("p (c i) t -> p c t i", i=4)
             src = m_raw[g][:, :, d0:d1].rearrange("p t (c i) -> p c t i", i=4)
             if engine == "s":
                 nc.scalar.copy(out=dst, in_=src)
             else:
                 nc.vector.tensor_copy(out=dst, in_=src)
+            if last:
+                load_m()
 
         def m_quantise(g):
-            q = work.tile([P, D], U32, name="m_codes%d" % g, tag="mq", bufs=6, align_bytes=64)
-            s = work.tile([P, D], U8, name="m_scales%d" % g, tag="ms", bufs=6, align_bytes=64)
+            q = work.tile([P, D], U32, name="m_codes%d" % g, tag="mq", bufs=8, align_bytes=64)
+            s = work.tile([P, D], U8, name="m_scales%d" % g, tag="ms", bufs=8, align_bytes=64)
             nc.vector.quantize_mx(
                 out=q[:].bitcast(FP8X4), scales=s[:], in_=m_grp[g][:].rearrange("p d j -> p (d j)")
             )
             m_codes[g] = q
             m_scales[g] = s
 
-        w_transpose(0)
-        w_copy_out(0)
-        w_quantise(0)
-        for c in range(N_CHUNKS):
-            if c + 3 < N_CHUNKS:
-                load_w(c + 3)
-            if c % 4 == 1 and c // 4 + 1 < 5:
-                load_m(c // 4 + 1)
-            if c % 4 == 0 and 2 <= c // 4 + 1 < 4:
-                load_bias(c // 4 + 1)
-            if c + 1 < N_CHUNKS:
-                w_transpose(c + 1)
-                w_copy_out(c + 1)
-            m_regroup(c // 4, "s", (c % 4) * 256, (c % 4 + 1) * 256)
-            if c + 1 < N_CHUNKS:
-                w_quantise(c + 1)
-            stage1(c)
-            if c % 4 == 3:
-                m_quantise(c // 4)
+        ready = []
 
-        nc.gpsimd.dma_start(out=gamma_bc[:], in_=ln_gamma.partition_broadcast(P))
-        nc.gpsimd.dma_start(out=beta_bc[:], in_=ln_beta.partition_broadcast(P))
+        def scalar_extras(n):
+            while n > 0:
+                if spread_bank():
+                    spread_bank()
+                elif state["pass"] < EARLY_PASSES:
+                    g = state["pass"]
+                    k = state["piece"]
+                    m_regroup(g, "s", k * 256, (k + 1) * 256, k == 3)
+                    if k == 3:
+                        ready.append(g)
+                        state["pass"] = g + 1
+                        state["piece"] = 0
+                    else:
+                        state["piece"] = k + 1
+                n -= 1
+
+        def quantise_ready():
+            while state["quantised"] < len(ready):
+                m_quantise(ready[state["quantised"]])
+                state["quantised"] = state["quantised"] + 1
+
+        for c in range(-2, N_CHUNKS):
+            if c + 2 < N_CHUNKS:
+                w_transpose_and_copy(c + 2)
+            if 0 <= c + 1 < N_CHUNKS:
+                w_quantise_and_multiply(c + 1)
+            if c >= 0:
+                add_bias_and_max(c)
+            if c == 0:
+                load_m()
+                load_m()
+            quantise_ready()
+            if c >= 0:
+                scalar_extras(1 if c + 2 < N_CHUNKS else 3)
+        quantise_ready()
 
         row_max = const.tile([P, T_TILES], F32, name="row_max")
         neg_max = const.tile([P, T_TILES], F32, name="neg_max")
         nc.vector.tensor_reduce(out=row_max[:], in_=chunk_max[:], axis=AX.X, op=ALU.max)
         nc.vector.tensor_scalar(out=neg_max[:], in0=row_max[:], scalar1=-1.0, scalar2=None, op0=ALU.mult)
 
+        e_codes = work.tile([P, N_UNITS * 512], U32, name="e_codes", tag="b16", bufs=1, align_bytes=64)
         acc = {}
         for a in range(T_TILES):
             for h in range(2):
                 acc[(a, h)] = psum.tile([P, 512], F32, name="acc%d_%d" % (a, h), tag="mm")
+        e_sb = {}
+        e_banks = {}
+        e_grp = {}
+
+        def exponentials(n):
+            t = raw_tile([P, T_TILES, UNIT], "e_sb%d" % n)
+            for a in range(T_TILES):
+                nc.scalar.activation(
+                    out=t[:, a, :],
+                    in_=logits[:, a, n * UNIT:(n + 1) * UNIT],
+                    func=ACT.Exp,
+                    bias=neg_max[:, a:a + 1],
+                    scale=1.0,
+                    accum_out=part_sum[:, a, n:n + 1],
+                )
+            e_sb[n] = t
+
+        def e_transpose(n):
+            banks = []
+            for k in range(2):
+                et = psum.tile([P, T_TILES, 4, P], BF16, name="et%d_%d" % (n, k), tag="tp")
+                for a in range(T_TILES):
+                    for j in range(4):
+                        lo = k * 512 + j * P
+                        nc.tensor.transpose(et[:, a, j, :], e_sb[n][:, a, lo:lo + P], ident_b[:])
+                banks.append(et)
+            e_banks[n] = banks
+
+        def e_copy_out(n):
+            t = grp_tile([P, 2, T_TILES, P, 4], BF16, "e_grp%d" % n)
+            for k in range(2):
+                nc.scalar.copy(out=t[:, k, :, :, :], in_=e_banks[n][k][:].rearrange("p a j t -> p a t j"))
+            e_grp[n] = t
+
+        def e_quantise(n):
+            nc.vector.quantize_mx(
+                out=e_codes[:, n * 512:(n + 1) * 512].bitcast(FP8X4),
+                scales=e_scales[:, n * 512:(n + 1) * 512],
+                in_=e_grp[n][:].rearrange("p k a t j -> p (k a t j)"),
+            )
 
         def stage2(g):
             for a in range(T_TILES):
@@ -236,73 +326,93 @@ def tile_probabilisticencoder_kernel(tc, enc_out, proj_w, proj_b, emb, ln_gamma,
                         stop=(g == N_PASSES - 1),
                     )
 
-        def late_pass(g):
-            if g + 1 < N_PASSES:
-                load_m(g + 1)
-            m_regroup(g, LATE_ENGINE[g - 4], 0, D)
-            m_quantise(g)
+        last_v = N_PASSES - LAST_ON_SCALAR
+        late = {"g": EARLY_PASSES, "q": EARLY_PASSES, "done": 0}
 
+        def vector_step():
+            if late["g"] < last_v:
+                g = late["g"]
+                m_regroup(g, "v", 0, 512, False)
+                m_regroup(g, "v", 512, 1024, True)
+                late["g"] = g + 1
+            if late["q"] < late["g"] and (late["g"] - late["q"] > 1 or late["g"] >= last_v):
+                m_quantise(late["q"])
+                late["q"] = late["q"] + 1
+
+        def multiply_up_to(limit):
+            while late["done"] < limit:
+                stage2(late["done"])
+                late["done"] = late["done"] + 1
+
+        exponentials(0)
+        exponentials(1)
+        e_transpose(0)
+        for i in range(PRE_STEPS):
+            vector_step()
         for n in range(N_UNITS):
-            e_sb = work.tile([P, T_TILES, UNIT], BF16, name="e_sb%d" % n, tag="e_sb", bufs=3)
-            for a in range(T_TILES):
-                nc.scalar.activation(
-                    out=e_sb[:, a, :],
-                    in_=logits[:, a, n * UNIT:(n + 1) * UNIT],
-                    func=ACT.Exp,
-                    bias=neg_max[:, a:a + 1],
-                    scale=1.0,
-                    accum_out=part_sum[:, a, n:n + 1],
-                )
-            e_grp = work.tile([P, 2, T_TILES, P, 4], BF16, name="e_grp%d" % n, tag="egrp", bufs=2, align_bytes=64)
-            for k in range(2):
-                et = psum.tile([P, T_TILES, 4, P], BF16, name="et%d_%d" % (n, k), tag="tp")
-                for a in range(T_TILES):
-                    for j in range(4):
-                        lo = k * 512 + j * P
-                        nc.tensor.transpose(et[:, a, j, :], e_sb[:, a, lo:lo + P], ident_b[:])
-                nc.scalar.copy(out=e_grp[:, k, :, :, :], in_=et[:].rearrange("p a j t -> p a t j"))
-            nc.vector.quantize_mx(
-                out=e_codes[:, n * 512:(n + 1) * 512].bitcast(FP8X4),
-                scales=e_scales[:, n * 512:(n + 1) * 512],
-                in_=e_grp[:].rearrange("p k a t j -> p (k a t j)"),
-            )
-            if n < 6:
-                late_pass(4 + 2 * n)
-                late_pass(5 + 2 * n)
-            stage2(2 * n)
-            stage2(2 * n + 1)
+            e_copy_out(n)
+            if n + 2 < N_UNITS:
+                exponentials(n + 2)
+            if n + 1 < N_UNITS:
+                e_transpose(n + 1)
+            e_quantise(n)
+            multiply_up_to(min(late["q"], 2 * n + 2))
+            for i in range(STEPS_PER_UNIT[n]):
+                vector_step()
+        for g in range(last_v, N_PASSES):
+            m_regroup(g, "s", 0, 512, False)
+            m_regroup(g, "s", 512, 1024, True)
+        while late["q"] < last_v:
+            vector_step()
+        for g in range(last_v, N_PASSES):
+            m_quantise(g)
+        multiply_up_to(N_PASSES)
 
         nc.scalar.activation(out=junk[:, 1:2], in_=part_sum[:, 1, N_UNITS - 1:N_UNITS], func=ACT.Sqrt)
-
         row_sum = const.tile([P, T_TILES], F32, name="row_sum")
         row_inv = const.tile([P, T_TILES], F32, name="row_inv")
         nc.vector.tensor_reduce(out=row_sum[:], in_=part_sum[:], axis=AX.X, op=ALU.add)
         nc.vector.reciprocal(out=row_inv[:], in_=row_sum[:])
 
+        y_sum = const.tile([P, T_TILES, 2], F32, name="y_sum")
+        mean_v = const.tile([P, T_TILES, 2], F32, name="mean_v")
+        sq_sum = const.tile([P, T_TILES], F32, name="sq_sum")
+        std = const.tile([P, T_TILES], F32, name="std")
+        rstd = const.tile([P, T_TILES], F32, name="rstd")
+        y = {}
+        o = {}
         for a in range(T_TILES):
-            y = work.tile([P, D], F32, name="y%d" % a, tag="grp", bufs=3, align_bytes=64)
-            stats = const.tile([P, 2, 6], F32, name="stats%d" % a)
-            mv = const.tile([P, 2], F32, name="mv%d" % a)
-            std = const.tile([P, 1], F32, name="std%d" % a)
-            rstd = const.tile([P, 1], F32, name="rstd%d" % a)
+            y[a] = grp_tile([P, D], F32, "y%d" % a)
             for h in range(2):
                 nc.vector.scalar_tensor_tensor(
-                    out=y[:, h * 512:(h + 1) * 512],
+                    out=y[a][:, h * 512:(h + 1) * 512],
                     in0=acc[(a, h)][:],
                     scalar=row_inv[:, a:a + 1],
                     in1=x_sb[:, a, h * 512:(h + 1) * 512],
                     op0=ALU.mult,
                     op1=ALU.add,
+                    accum_out=y_sum[:, a, h:h + 1],
                 )
-                nc.vector.bn_stats(out=stats[:, h, :], in_=y[:, h * 512:(h + 1) * 512])
-            nc.vector.bn_aggr(out=mv[:], in_=stats[:].rearrange("p h s -> p (h s)"))
-            nc.scalar.activation(out=std[:], in_=mv[:, 1:2], func=ACT.Sqrt, bias=small[:, 1:2], scale=1.0)
-            nc.vector.reciprocal(out=rstd[:], in_=std[:])
-            o = work.tile([P, D], F32, name="o%d" % a, tag="grp", bufs=3, align_bytes=64)
-            nc.vector.scalar_tensor_tensor(
-                out=o[:], in0=y[:], scalar=mv[:, 0:1], in1=gamma_bc[:], op0=ALU.subtract, op1=ALU.mult
+            nc.vector.tensor_reduce(out=mean_v[:, a, 0:1], in_=y_sum[:, a, :], axis=AX.X, op=ALU.add)
+            nc.vector.tensor_scalar(
+                out=mean_v[:, a, 1:2], in0=mean_v[:, a, 0:1], scalar1=-1.0 / D, scalar2=None, op0=ALU.mult
             )
-            nc.vector.scalar_tensor_tensor(
-                out=o[:], in0=o[:], scalar=rstd[:, 0:1], in1=beta_bc[:], op0=ALU.mult, op1=ALU.add
+        for a in range(T_TILES):
+            sq = raw_tile([P, D], "sq%d" % a)
+            nc.scalar.activation(
+                out=sq[:], in_=y[a][:], func=ACT.Square, bias=mean_v[:, a, 1:2], scale=1.0,
+                accum_out=sq_sum[:, a:a + 1],
             )
-            nc.sync.dma_start(out=out_dram[a * P:(a + 1) * P, :], in_=o[:])
+            nc.scalar.activation(
+                out=std[:, a:a + 1], in_=sq_sum[:, a:a + 1], func=ACT.Sqrt, bias=small[:, 1:2], scale=1.0 / D
+            )
+            o[a] = grp_tile([P, D], F32, "o%d" % a)
+            nc.vector.scalar_tensor_tensor(
+                out=o[a][:], in0=y[a][:], scalar=mean_v[:, a, 1:2], in1=gb_bc[:, 0, :], op0=ALU.add, op1=ALU.mult
+            )
+        for a in range(T_TILES):
+            nc.vector.reciprocal(out=rstd[:, a:a + 1], in_=std[:, a:a + 1])
+            nc.vector.scalar_tensor_tensor(
+                out=o[a][:], in0=o[a][:], scalar=rstd[:, a:a + 1], in1=gb_bc[:, 1, :], op0=ALU.mult, op1=ALU.add
+            )
+            nc.sync.dma_start(out=out_dram[a * P:(a + 1) * P, :], in_=o[a][:])

@@ -25,7 +25,7 @@ LN_EPS = 1e-5
 
 FLOPS = 2 * 2 * 256 * V * D
 
-PINNED = True
+PINNED = False
 EARLY_PASSES = 4
 FIRST_BIAS_BANKS = 3
 PRE_STEPS = 3

@@ -52,7 +52,6 @@ def tile_probabilisticencoder_kernel(tc, enc_out, proj_w, proj_b, emb, ln_gamma,
             return work.tile(shape, dtype, name=name, tag="grp", bufs=4, align_bytes=64)
 
         x_sb = const.tile([P, T_TILES, D], BF16, name="x_sb")
-        nc.sync.dma_start(out=x_sb[:], in_=x_dram.rearrange("(a p) d -> p a d", p=P))
 
         rows = const.tile([P, CHUNK], BF16, name="rows")
         nc.vector.memset(rows[:], 0.0)
@@ -85,9 +84,12 @@ def tile_probabilisticencoder_kernel(tc, enc_out, proj_w, proj_b, emb, ln_gamma,
 
         def load_w(c):
             t = raw_tile([P, 4, D], "w_raw%d" % c)
-            nc.sync.dma_start(
-                out=t[:], in_=proj_w[c * CHUNK:(c + 1) * CHUNK, :].rearrange("(q i) k -> q i k", i=4)
-            )
+            src = proj_w[c * CHUNK:(c + 1) * CHUNK, :].rearrange("(q i) k -> q i k", i=4)
+            if c == 0:
+                for i in range(4):
+                    nc.sync.dma_start(out=t[:, i, :], in_=src[:, i, :])
+            else:
+                nc.sync.dma_start(out=t[:], in_=src)
             w_raw[c] = t
 
         def load_m():
@@ -101,6 +103,7 @@ def tile_probabilisticencoder_kernel(tc, enc_out, proj_w, proj_b, emb, ln_gamma,
                 state["next_m"] = g + 1
 
         load_w(0)
+        nc.sync.dma_start(out=x_sb[:], in_=x_dram.rearrange("(a p) d -> p a d", p=P))
         load_w(1)
         load_w(2)
 
@@ -332,8 +335,7 @@ def tile_probabilisticencoder_kernel(tc, enc_out, proj_w, proj_b, emb, ln_gamma,
         def vector_step():
             if late["g"] < last_v:
                 g = late["g"]
-                m_regroup(g, "v", 0, 512, False)
-                m_regroup(g, "v", 512, 1024, True)
+                m_regroup(g, "v", 0, D, True)
                 late["g"] = g + 1
             if late["q"] < late["g"] and (late["g"] - late["q"] > 1 or late["g"] >= last_v):
                 m_quantise(late["q"])
@@ -412,7 +414,10 @@ def tile_probabilisticencoder_kernel(tc, enc_out, proj_w, proj_b, emb, ln_gamma,
             )
         for a in range(T_TILES):
             nc.vector.reciprocal(out=rstd[:, a:a + 1], in_=std[:, a:a + 1])
-            nc.vector.scalar_tensor_tensor(
-                out=o[a][:], in0=o[a][:], scalar=rstd[:, a:a + 1], in1=gb_bc[:, 1, :], op0=ALU.mult, op1=ALU.add
-            )
-            nc.sync.dma_start(out=out_dram[a * P:(a + 1) * P, :], in_=o[a][:])
+            for h in range(2):
+                cols = slice(h * 512, (h + 1) * 512)
+                nc.vector.scalar_tensor_tensor(
+                    out=o[a][:, cols], in0=o[a][:, cols], scalar=rstd[:, a:a + 1], in1=gb_bc[:, 1, cols],
+                    op0=ALU.mult, op1=ALU.add,
+                )
+                nc.sync.dma_start(out=out_dram[a * P:(a + 1) * P, cols], in_=o[a][:, cols])

from contextlib import ExitStack

import concourse.mybir as mybir
from concourse.masks import make_identity

F32 = mybir.dt.float32
BF16 = mybir.dt.bfloat16
U32 = mybir.dt.uint32
U8 = mybir.dt.uint8
FP8X4 = mybir.dt.float8_e4m3fn_x4
ALU = mybir.AluOpType
ACT = mybir.ActivationFunctionType
AX = mybir.AxisListType

P = 128
T_TILES = 2
D = 1024
V = 8192
CHUNK = 512
N_CHUNKS = V // CHUNK
N_PASSES = V // 512
UNIT = 1024
N_UNITS = V // UNIT
LN_EPS = 1e-5

FLOPS = 2 * 2 * 256 * V * D

PINNED = False
EARLY_PASSES = 4
FIRST_BIAS_BANKS = 3
PRE_STEPS = 3
STEPS_PER_UNIT = [1, 1, 1, 2, 1, 1, 1, 1]
LAST_ON_SCALAR = 1


def tile_probabilisticencoder_kernel(tc, enc_out, proj_w, proj_b, emb, ln_gamma, ln_beta, out):
    nc = tc.nc
    x_dram = enc_out.flatten_outer_dims()
    out_dram = out.flatten_outer_dims()

    with ExitStack() as ctx:
        const = ctx.enter_context(tc.tile_pool(name="const", bufs=1))
        work = ctx.enter_context(tc.tile_pool(name="work", bufs=2))
        psum = ctx.enter_context(tc.psum_pool(name="psum", bufs=4))
        if PINNED:
            ctx.enter_context(tc.manual_schedule())

        def raw_tile(shape, name):
            return work.tile(shape, BF16, name=name, tag="raw", bufs=6, align_bytes=64)

        def grp_tile(shape, dtype, name):
            return work.tile(shape, dtype, name=name, tag="grp", bufs=4, align_bytes=64)

        x_sb = const.tile([P, T_TILES, D], BF16, name="x_sb")

        rows = const.tile([P, CHUNK], BF16, name="rows")
        nc.vector.memset(rows[:], 0.0)
        nc.scalar.dma_start(out=rows[0:16, :], in_=proj_b.rearrange("(c n) -> c n", n=CHUNK))
        nc.scalar.dma_start(out=rows[16:18, :], in_=ln_gamma.rearrange("(c n) -> c n", n=CHUNK))
        nc.scalar.dma_start(out=rows[18:20, :], in_=ln_beta.rearrange("(c n) -> c n", n=CHUNK))
        ident_f = const.tile([P, P], F32, name="ident_f")
        make_identity(nc, ident_f[:])
        ident_b = const.tile([P, P], BF16, name="ident_b")
        make_identity(nc, ident_b[:])

        small = const.tile([P, 2], F32, name="small")
        nc.vector.memset(small[:, 0:1], 0.0)
        nc.vector.memset(small[:, 1:2], LN_EPS)
        junk = const.tile([P, 2], F32, name="junk")
        nc.scalar.activation(out=junk[:, 0:1], in_=small[:, 0:1], func=ACT.Exp)

        logits = const.tile([P, T_TILES, V], F32, name="logits")
        chunk_max = const.tile([P, T_TILES, N_CHUNKS], F32, name="chunk_max")
        part_sum = const.tile([P, T_TILES, N_UNITS], F32, name="part_sum")
        e_scales = const.tile([P, N_UNITS * 512], U8, name="e_scales", align_bytes=64)
        x_codes = const.tile([P, 512], U32, name="x_codes", align_bytes=64)
        x_scales = const.tile([P, 512], U8, name="x_scales", align_bytes=64)
        gb_bc = const.tile([P, 2, D], BF16, name="gb_bc")
        bias_bc = work.tile([P, V], BF16, name="bias_bc", tag="b16", bufs=1, align_bytes=64)

        w_raw = {}
        m_raw = {}
        state = {"next_m": 0, "bias": 0, "pass": 0, "piece": 0, "quantised": 0}

        def load_w(c):
            t = raw_tile([P, 4, D], "w_raw%d" % c)
            src = proj_w[c * CHUNK:(c + 1) * CHUNK, :].rearrange("(q i) k -> q i k", i=4)
            if c == 0:
                for i in range(4):
                    nc.sync.dma_start(out=t[:, i, :], in_=src[:, i, :])
            else:
                nc.sync.dma_start(out=t[:], in_=src)
            w_raw[c] = t

        def load_m():
            g = state["next_m"]
            if g < N_PASSES:
                t = raw_tile([P, 4, D], "m_raw%d" % g)
                nc.sync.dma_start(
                    out=t[:], in_=emb[g * 512:(g + 1) * 512, :].rearrange("(p j) d -> p j d", j=4)
                )
                m_raw[g] = t
                state["next_m"] = g + 1

        load_w(0)
        nc.sync.dma_start(out=x_sb[:], in_=x_dram.rearrange("(a p) d -> p a d", p=P))
        load_w(1)
        load_w(2)

        x_grp = grp_tile([P, 2, T_TILES, P, 4], BF16, "x_grp")
        x_grp32 = x_grp[:].bitcast(F32)
        for a in range(T_TILES):
            xt = psum.tile([P, 4, P], F32, name="xt%d" % a, tag="tp")
            xw = x_sb[:, a, :].bitcast(F32)
            for u in range(4):
                nc.tensor.transpose(xt[:, u, :], xw[:, u * P:(u + 1) * P], ident_f[:])
            nc.scalar.copy(out=x_grp32[:, :, a, :, :], in_=xt[:].rearrange("p (g u) t -> p g t u", g=2))
        nc.vector.quantize_mx(
            out=x_codes[:].bitcast(FP8X4),
            scales=x_scales[:],
            in_=x_grp[:].rearrange("p g a t j -> p (g a t j)"),
        )

        def spread_bank():
            r = state["bias"]
            if r >= 10:
                return False
            bank = psum.tile([P, 2 * CHUNK], BF16, name="bank%d" % r, tag="mm")
            for h in range(2):
                row = 2 * r + h
                nc.tensor.matmul(
                    out=bank[:, h * CHUNK:(h + 1) * CHUNK],
                    lhsT=ident_b[:, row:row + 1].to_broadcast([P, P]),
                    rhs=rows[:],
                    start=True,
                    stop=True,
                )
            if r < 8:
                nc.scalar.copy(out=bias_bc[:, r * 1024:(r + 1) * 1024], in_=bank[:])
            else:
                nc.scalar.copy(out=gb_bc[:, r - 8, :], in_=bank[:])
            state["bias"] = r + 1
            return True

        for r in range(FIRST_BIAS_BANKS):
            spread_bank()

        w_grp = {}
        w_codes = {}
        w_scales = {}
        lg = {}

        def w_transpose_and_copy(c):
            banks = []
            for i in range(4):
                tp = psum.tile([P, 4, P], F32, name="wt%d_%d" % (c, i), tag="tp")
                ww = w_raw[c][:, i, :].bitcast(F32)
                for u in range(4):
                    nc.tensor.transpose(tp[:, u, :], ww[:, u * P:(u + 1) * P], ident_f[:])
                banks.append(tp)
            if c + 3 < N_CHUNKS:
                load_w(c + 3)
            g = grp_tile([P, 2, CHUNK, 4], BF16, "w_grp%d" % c)
            g32 = g[:].bitcast(F32)
            for i in range(4):
                nc.scalar.copy(
                    out=g32[:, :, i * P:(i + 1) * P, :],
                    in_=banks[i][:].rearrange("p (g u) q -> p g q u", g=2),
                )
            w_grp[c] = g

        def w_quantise_and_multiply(c):
            q = work.tile([P, 2 * CHUNK], U32, name="w_codes%d" % c, tag="wq", bufs=2, align_bytes=64)
            s = work.tile([P, 2 * CHUNK], U8, name="w_scales%d" % c, tag="ws", bufs=2, align_bytes=64)
            nc.vector.quantize_mx(
                out=q[:].bitcast(FP8X4), scales=s[:], in_=w_grp[c][:].rearrange("p g v j -> p (g v j)")
            )
            for a in range(T_TILES):
                t = psum.tile([P, CHUNK], F32, name="lg%d_%d" % (c, a), tag="mm")
                for g in range(2):
                    lo = (g * T_TILES + a) * P
                    nc.tensor.matmul_mx(
                        out=t[:],
                        lhsT=x_codes[:, lo:lo + P].bitcast(FP8X4),
                        lhsT_scale=x_scales[:, lo:lo + P],
                        rhs=q[:, g * CHUNK:(g + 1) * CHUNK].bitcast(FP8X4),
                        rhs_scale=s[:, g * CHUNK:(g + 1) * CHUNK],
                        start=(g == 0),
                        stop=(g == 1),
                    )
                lg[(c, a)] = t

        def add_bias_and_max(c):
            cols = slice(c * CHUNK, (c + 1) * CHUNK)
            for a in range(T_TILES):
                nc.vector.tensor_tensor(
                    out=logits[:, a, cols].rearrange("p (i q) -> p i q", i=4),
                    in0=lg[(c, a)][:].rearrange("p (i q) -> p i q", i=4),
                    in1=bias_bc[:, cols].rearrange("p (q i) -> p i q", i=4),
                    op=ALU.add,
                )
            nc.vector.tensor_reduce(out=chunk_max[:, :, c], in_=logits[:, :, cols], axis=AX.X, op=ALU.max)

        m_grp = {}
        m_codes = {}
        m_scales = {}

        def m_regroup(g, engine, d0, d1, last):
            if g not in m_grp:
                m_grp[g] = grp_tile([P, D, 4], BF16, "m_grp%d" % g)
            dst = m_grp[g][:, d0:d1, :].rearrange("p (c i) t -> p c t i", i=4)
            src = m_raw[g][:, :, d0:d1].rearrange("p t (c i) -> p c t i", i=4)
            if engine == "s":
                nc.scalar.copy(out=dst, in_=src)
            else:
                nc.vector.tensor_copy(out=dst, in_=src)
            if last:
                load_m()

        def m_quantise(g):
            q = work.tile([P, D], U32, name="m_codes%d" % g, tag="mq", bufs=8, align_bytes=64)
            s = work.tile([P, D], U8, name="m_scales%d" % g, tag="ms", bufs=8, align_bytes=64)
            nc.vector.quantize_mx(
                out=q[:].bitcast(FP8X4), scales=s[:], in_=m_grp[g][:].rearrange("p d j -> p (d j)")
            )
            m_codes[g] = q
            m_scales[g] = s

        ready = []

        def scalar_extras(n):
            while n > 0:
                if spread_bank():
                    spread_bank()
                elif state["pass"] < EARLY_PASSES:
                    g = state["pass"]
                    k = state["piece"]
                    m_regroup(g, "s", k * 256, (k + 1) * 256, k == 3)
                    if k == 3:
                        ready.append(g)
                        state["pass"] = g + 1
                        state["piece"] = 0
                    else:
                        state["piece"] = k + 1
                n -= 1

        def quantise_ready():
            while state["quantised"] < len(ready):
                m_quantise(ready[state["quantised"]])
                state["quantised"] = state["quantised"] + 1

        for c in range(-2, N_CHUNKS):
            if c + 2 < N_CHUNKS:
                w_transpose_and_copy(c + 2)
            if 0 <= c + 1 < N_CHUNKS:
                w_quantise_and_multiply(c + 1)
            if c >= 0:
                add_bias_and_max(c)
            if c == 0:
                load_m()
                load_m()
            quantise_ready()
            if c >= 0:
                scalar_extras(1 if c + 2 < N_CHUNKS else 3)
        quantise_ready()

        row_max = const.tile([P, T_TILES], F32, name="row_max")
        neg_max = const.tile([P, T_TILES], F32, name="neg_max")
        nc.vector.tensor_reduce(out=row_max[:], in_=chunk_max[:], axis=AX.X, op=ALU.max)
        nc.vector.tensor_scalar(out=neg_max[:], in0=row_max[:], scalar1=-1.0, scalar2=None, op0=ALU.mult)

        e_codes = work.tile([P, N_UNITS * 512], U32, name="e_codes", tag="b16", bufs=1, align_bytes=64)
        acc = {}
        for a in range(T_TILES):
            for h in range(2):
                acc[(a, h)] = psum.tile([P, 512], F32, name="acc%d_%d" % (a, h), tag="mm")
        e_sb = {}
        e_banks = {}
        e_grp = {}

        def exponentials(n):
            t = raw_tile([P, T_TILES, UNIT], "e_sb%d" % n)
            for a in range(T_TILES):
                nc.scalar.activation(
                    out=t[:, a, :],
                    in_=logits[:, a, n * UNIT:(n + 1) * UNIT],
                    func=ACT.Exp,
                    bias=neg_max[:, a:a + 1],
                    scale=1.0,
                    accum_out=part_sum[:, a, n:n + 1],
                )
            e_sb[n] = t

        def e_transpose(n):
            banks = []
            for k in range(2):
                et = psum.tile([P, T_TILES, 4, P], BF16, name="et%d_%d" % (n, k), tag="tp")
                for a in range(T_TILES):
                    for j in range(4):
                        lo = k * 512 + j * P
                        nc.tensor.transpose(et[:, a, j, :], e_sb[n][:, a, lo:lo + P], ident_b[:])
                banks.append(et)
            e_banks[n] = banks

        def e_copy_out(n):
            t = grp_tile([P, 2, T_TILES, P, 4], BF16, "e_grp%d" % n)
            for k in range(2):
                nc.scalar.copy(out=t[:, k, :, :, :], in_=e_banks[n][k][:].rearrange("p a j t -> p a t j"))
            e_grp[n] = t

        def e_quantise(n):
            nc.vector.quantize_mx(
                out=e_codes[:, n * 512:(n + 1) * 512].bitcast(FP8X4),
                scales=e_scales[:, n * 512:(n + 1) * 512],
                in_=e_grp[n][:].rearrange("p k a t j -> p (k a t j)"),
            )

        def stage2(g):
            for a in range(T_TILES):
                lo = (g * T_TILES + a) * P
                for h in range(2):
                    nc.tensor.matmul_mx(
                        out=acc[(a, h)][:],
                        lhsT=e_codes[:, lo:lo + P].bitcast(FP8X4),
                        lhsT_scale=e_scales[:, lo:lo + P],
                        rhs=m_codes[g][:, h * 512:(h + 1) * 512].bitcast(FP8X4),
                        rhs_scale=m_scales[g][:, h * 512:(h + 1) * 512],
                        start=(g == 0),
                        stop=(g == N_PASSES - 1),
                    )

        last_v = N_PASSES - LAST_ON_SCALAR
        late = {"g": EARLY_PASSES, "q": EARLY_PASSES, "done": 0}

        def vector_step():
            if late["g"] < last_v:
                g = late["g"]
                m_regroup(g, "v", 0, D, True)
                late["g"] = g + 1
            if late["q"] < late["g"] and (late["g"] - late["q"] > 1 or late["g"] >= last_v):
                m_quantise(late["q"])
                late["q"] = late["q"] + 1

        def multiply_up_to(limit):
            while late["done"] < limit:
                stage2(late["done"])
                late["done"] = late["done"] + 1

        exponentials(0)
        exponentials(1)
        e_transpose(0)
        for i in range(PRE_STEPS):
            vector_step()
        for n in range(N_UNITS):
            e_copy_out(n)
            if n + 2 < N_UNITS:
                exponentials(n + 2)
            if n + 1 < N_UNITS:
                e_transpose(n + 1)
            e_quantise(n)
            multiply_up_to(min(late["q"], 2 * n + 2))
            for i in range(STEPS_PER_UNIT[n]):
                vector_step()
        for g in range(last_v, N_PASSES):
            m_regroup(g, "s", 0, 512, False)
            m_regroup(g, "s", 512, 1024, True)
        while late["q"] < last_v:
            vector_step()
        for g in range(last_v, N_PASSES):
            m_quantise(g)
        multiply_up_to(N_PASSES)

        nc.scalar.activation(out=junk[:, 1:2], in_=part_sum[:, 1, N_UNITS - 1:N_UNITS], func=ACT.Sqrt)
        row_sum = const.tile([P, T_TILES], F32, name="row_sum")
        row_inv = const.tile([P, T_TILES], F32, name="row_inv")
        nc.vector.tensor_reduce(out=row_sum[:], in_=part_sum[:], axis=AX.X, op=ALU.add)
        nc.vector.reciprocal(out=row_inv[:], in_=row_sum[:])

        y_sum = const.tile([P, T_TILES, 2], F32, name="y_sum")
        mean_v = const.tile([P, T_TILES, 2], F32, name="mean_v")
        sq_sum = const.tile([P, T_TILES], F32, name="sq_sum")
        std = const.tile([P, T_TILES], F32, name="std")
        rstd = const.tile([P, T_TILES], F32, name="rstd")
        y = {}
        o = {}
        for a in range(T_TILES):
            y[a] = grp_tile([P, D], F32, "y%d" % a)
            for h in range(2):
                nc.vector.scalar_tensor_tensor(
                    out=y[a][:, h * 512:(h + 1) * 512],
                    in0=acc[(a, h)][:],
                    scalar=row_inv[:, a:a + 1],
                    in1=x_sb[:, a, h * 512:(h + 1) * 512],
                    op0=ALU.mult,
                    op1=ALU.add,
                    accum_out=y_sum[:, a, h:h + 1],
                )
            nc.vector.tensor_reduce(out=mean_v[:, a, 0:1], in_=y_sum[:, a, :], axis=AX.X, op=ALU.add)
            nc.vector.tensor_scalar(
                out=mean_v[:, a, 1:2], in0=mean_v[:, a, 0:1], scalar1=-1.0 / D, scalar2=None, op0=ALU.mult
            )
        for a in range(T_TILES):
            sq = raw_tile([P, D], "sq%d" % a)
            nc.scalar.activation(
                out=sq[:], in_=y[a][:], func=ACT.Square, bias=mean_v[:, a, 1:2], scale=1.0,
                accum_out=sq_sum[:, a:a + 1],
            )
            nc.scalar.activation(
                out=std[:, a:a + 1], in_=sq_sum[:, a:a + 1], func=ACT.Sqrt, bias=small[:, 1:2], scale=1.0 / D
            )
            o[a] = grp_tile([P, D], F32, "o%d" % a)
            nc.vector.scalar_tensor_tensor(
                out=o[a][:], in0=y[a][:], scalar=mean_v[:, a, 1:2], in1=gb_bc[:, 0, :], op0=ALU.add, op1=ALU.mult
            )
        for a in range(T_TILES):
            nc.vector.reciprocal(out=rstd[:, a:a + 1], in_=std[:, a:a + 1])
            for h in range(2):
                cols = slice(h * 512, (h + 1) * 512)
                nc.vector.scalar_tensor_tensor(
                    out=o[a][:, cols], in0=o[a][:, cols], scalar=rstd[:, a:a + 1], in1=gb_bc[:, 1, cols],
                    op0=ALU.mult, op1=ALU.add,
                )
                nc.sync.dma_start(out=out_dram[a * P:(a + 1) * P, cols], in_=o[a][:, cols])
